import numpy as np
import ml_dtypes


def mxq(x, axis, fmt="e4m3"):
    dtype, down = {"e4m3": (ml_dtypes.float8_e4m3fn, 7), "e5m2": (ml_dtypes.float8_e5m2, 14)}[fmt]
    v = np.moveaxis(np.asarray(x, np.float32).astype(ml_dtypes.bfloat16).astype(np.float64), axis, -1)
    blocks = v.reshape(v.shape[:-1] + (-1, 32))
    amax = np.abs(blocks).max(-1, keepdims=True)
    byte = np.maximum(np.where(amax > 0, np.frexp(amax)[1] - 1 + 127, 0) - down, 1)
    scale = np.exp2(byte - 127.0)
    codes = (blocks / scale).astype(np.float32).astype(dtype).astype(np.float64)
    return np.moveaxis((codes * scale).reshape(v.shape), -1, axis)


WIDE = False


def mx_kscale(k):
    if not WIDE:
        return np.ones(k)
    levels = np.array([10, -10, 5, -5, 0])
    a = np.random.permutation(np.resize(levels, k // 512 * 4)).reshape(k // 512, 4)
    idx = np.arange(k)
    return np.exp2(a[idx // 512, idx % 128 // 32])


BF16 = ml_dtypes.bfloat16


def bf(x):
    return np.asarray(x, np.float32).astype(BF16)


def f64(x):
    return np.asarray(x).astype(np.float64)


B, T, HID, H, NOPE, ROPE, VD, KV_LORA = 4, 2048, 512, 4, 64, 64, 128, 512
QK = NOPE + ROPE
HALF = ROPE // 2


def rope(x, cos, sin):
    c = cos[None, :, None, :]
    s = sin[None, :, None, :]
    x1, x2 = x[..., 0::2], x[..., 1::2]
    o1 = x1 * c - x2 * s
    o2 = x1 * s + x2 * c
    return np.stack([o1, o2], axis=-1).reshape(x.shape)


def setup_inputs():
    s = mx_kscale(HID)
    ang = np.random.uniform(-np.pi, np.pi, (T, HALF))
    return {"hidden_states": bf(np.random.standard_normal((B, T, HID)) * s),
            "rope_cos": bf(np.cos(ang)), "rope_sin": bf(np.sin(ang)),
            "Wq": bf(np.random.standard_normal((HID, H * QK)) / np.sqrt(HID) / s[:, None])}


def reference(hidden_states, rope_cos, rope_sin, Wq):
    q = (mxq(f64(hidden_states), 2, "e4m3") @ mxq(f64(Wq), 0, "e4m3")).reshape(B, T, H, QK)
    q_nope, q_rope = q[..., :NOPE], q[..., NOPE:]
    q_rope = rope(q_rope, f64(rope_cos), f64(rope_sin))
    return np.concatenate([q_nope, q_rope], axis=-1)

@@ -1,0 +1,181 @@
+from contextlib import ExitStack
+
+import concourse.mybir as mybir
+from concourse.masks import make_identity
+
+F32 = mybir.dt.float32
+BF16 = mybir.dt.bfloat16
+U32 = mybir.dt.uint32
+U8 = mybir.dt.uint8
+FP8X4 = mybir.dt.float8_e4m3fn_x4
+MULT = mybir.AluOpType.mult
+ADD = mybir.AluOpType.add
+
+P = 128
+PACK = 4
+BATCH, TOKENS, HID = 4, 2048, 512
+HEADS, HEAD_DIM = 4, 128
+NOPE = 64
+PAIRS = 32
+COLS = HEADS * HEAD_DIM
+PLAIN_COLS = HEADS * NOPE
+PLANE = HEADS * PAIRS
+TILES_PER_BATCH = TOKENS // P
+STEP_TILES = 2
+STEPS_PER_BATCH = TILES_PER_BATCH // STEP_TILES
+STEPS = BATCH * STEPS_PER_BATCH
+LOAD_TILES = 4
+STEPS_PER_LOAD = LOAD_TILES // STEP_TILES
+LOADS = BATCH * TILES_PER_BATCH // LOAD_TILES
+WORDS = HID // 2
+
+FLOPS = 2 * BATCH * TOKENS * HID * COLS
+
+
+def tile_multilatentattention_pb_t_kernel(tc, hidden_states, rope_cos, rope_sin, Wq, out):
+    nc = tc.nc
+    x_view = hidden_states.rearrange("b (p j) k -> b p j k", p=P)
+    out_view = out.rearrange("b (p j) h d -> b p j (h d)", p=P)
+
+    with ExitStack() as ctx:
+        const = ctx.enter_context(tc.tile_pool(name="const", bufs=1))
+        x_pool = ctx.enter_context(tc.tile_pool(name="x", bufs=LOADS))
+        grouped_pool = ctx.enter_context(tc.tile_pool(name="grouped", bufs=3))
+        mx_pool = ctx.enter_context(tc.tile_pool(name="mx", bufs=3))
+        product_pool = ctx.enter_context(tc.tile_pool(name="product", bufs=3))
+        out_pool = ctx.enter_context(tc.tile_pool(name="result", bufs=8))
+        xt_pool = ctx.enter_context(tc.psum_pool(name="xt", bufs=2))
+        plain_pool = ctx.enter_context(tc.psum_pool(name="plain", bufs=3))
+        rope_pool = ctx.enter_context(tc.psum_pool(name="rope", bufs=3))
+
+        def load_tokens(load):
+            b, j0 = divmod(load * LOAD_TILES, TILES_PER_BATCH)
+            x_sb = x_pool.tile([P, LOAD_TILES * HID], BF16)
+            nc.sync.dma_start(
+                out=x_sb[:], in_=x_view[b, :, j0 : j0 + LOAD_TILES, :].rearrange("p j k -> p (j k)")
+            )
+            return x_sb
+
+        x_tiles = [load_tokens(0)]
+        w_raw = const.tile([P, PACK, COLS], BF16)
+        nc.sync.dma_start(
+            out=w_raw[:].rearrange("q (u e) c -> q u e c", u=2),
+            in_=Wq.rearrange("(u q e) c -> q u e c", u=2, e=2),
+        )
+        cos_sb = const.tile([P, TILES_PER_BATCH, PAIRS], BF16)
+        nc.sync.dma_start(out=cos_sb[:], in_=rope_cos.rearrange("(p j) i -> p j i", p=P))
+        sin_sb = const.tile([P, TILES_PER_BATCH, PAIRS], BF16)
+        nc.sync.dma_start(out=sin_sb[:], in_=rope_sin.rearrange("(p j) i -> p j i", p=P))
+        for load in range(1, LOADS):
+            x_tiles.append(load_tokens(load))
+
+        ident = const.tile([P, P], F32)
+        make_identity(nc, ident[:])
+
+        w_grouped = const.tile([P, COLS, PACK], BF16, align_bytes=64)
+        nc.vector.tensor_copy(
+            out=w_grouped[:, 0:PLAIN_COLS, :].rearrange("q (h d) t -> q h d t", h=HEADS),
+            in_=w_raw[:].rearrange("q t (h z d) -> q z h d t", h=HEADS, z=2)[:, 0],
+        )
+        for e in range(2):
+            first = PLAIN_COLS + e * PLANE
+            nc.vector.tensor_copy(
+                out=w_grouped[:, first : first + PLANE, :].rearrange("q (h i) t -> q h i t", h=HEADS),
+                in_=w_raw[:].rearrange("q t (h z i e) -> q z e h i t", h=HEADS, z=2, e=2)[:, 1, e],
+            )
+        w_codes = const.tile([P, COLS], U32, align_bytes=64)
+        w_scales = const.tile([P, COLS], U8, align_bytes=64)
+        nc.vector.quantize_mx(
+            out=w_codes[:].bitcast(FP8X4),
+            scales=w_scales[:],
+            in_=w_grouped[:].rearrange("q c t -> q (c t)"),
+        )
+
+        even_factors = const.tile([P, STEPS_PER_BATCH, 2, STEP_TILES, PAIRS], BF16)
+        odd_factors = const.tile([P, STEPS_PER_BATCH, 2, STEP_TILES, PAIRS], BF16)
+        cos_by_step = cos_sb[:].rearrange("p (s t) i -> p s t i", t=STEP_TILES)
+        sin_by_step = sin_sb[:].rearrange("p (s t) i -> p s t i", t=STEP_TILES)
+        nc.vector.tensor_copy(out=even_factors[:, :, 0, :, :], in_=cos_by_step)
+        nc.vector.tensor_copy(out=even_factors[:, :, 1, :, :], in_=sin_by_step)
+        nc.vector.tensor_scalar_mul(out=odd_factors[:, :, 0, :, :], in0=sin_by_step, scalar1=-1.0)
+        nc.vector.tensor_copy(out=odd_factors[:, :, 1, :, :], in_=cos_by_step)
+
+        def transpose_and_quantise(step):
+            words = x_tiles[step // STEPS_PER_LOAD][:].bitcast(F32)
+            first_word = (step % STEPS_PER_LOAD) * STEP_TILES * WORDS
+            xt = xt_pool.tile([P, STEP_TILES, 2, P], F32)
+            for t in range(STEP_TILES):
+                for u in range(2):
+                    start = first_word + (2 * t + u) * P
+                    nc.tensor.transpose(xt[:, t, u, :], words[:, start : start + P], ident[:])
+            grouped = grouped_pool.tile([P, STEP_TILES * P * PACK], BF16, align_bytes=64)
+            nc.scalar.copy(
+                out=grouped[:].bitcast(F32).rearrange("q (t n u) -> q t n u", t=STEP_TILES, u=2),
+                in_=xt[:].rearrange("q t u n -> q t n u"),
+            )
+            x_codes = mx_pool.tile([P, STEP_TILES * P], U32, align_bytes=64)
+            x_scales = mx_pool.tile([P, STEP_TILES * P], U8, align_bytes=64)
+            nc.vector.quantize_mx(out=x_codes[:].bitcast(FP8X4), scales=x_scales[:], in_=grouped[:])
+            return x_codes, x_scales
+
+        def project_and_rotate(step, x_codes, x_scales):
+            b, step_in_batch = divmod(step, STEPS_PER_BATCH)
+            plain = plain_pool.tile([P, STEP_TILES, PLAIN_COLS], F32)
+            rope = rope_pool.tile([P, STEP_TILES, 2, PLANE], F32)
+            for t in range(STEP_TILES):
+                tokens = slice(t * P, (t + 1) * P)
+                nc.tensor.matmul_mx(
+                    out=plain[:, t, :],
+                    lhsT=x_codes[:, tokens].bitcast(FP8X4),
+                    lhsT_scale=x_scales[:, tokens],
+                    rhs=w_codes[:, 0:PLAIN_COLS].bitcast(FP8X4),
+                    rhs_scale=w_scales[:, 0:PLAIN_COLS],
+                    start=True,
+                    stop=True,
+                )
+                nc.tensor.matmul_mx(
+                    out=rope[:, t, :, :].rearrange("p e c -> p (e c)"),
+                    lhsT=x_codes[:, tokens].bitcast(FP8X4),
+                    lhsT_scale=x_scales[:, tokens],
+                    rhs=w_codes[:, PLAIN_COLS:COLS].bitcast(FP8X4),
+                    rhs_scale=w_scales[:, PLAIN_COLS:COLS],
+                    start=True,
+                    stop=True,
+                )
+
+            result = out_pool.tile([P, STEP_TILES, HEADS, HEAD_DIM], F32)
+            nc.scalar.copy(
+                out=result[:, :, :, 0:NOPE],
+                in_=plain[:].rearrange("p t (h d) -> p t h d", h=HEADS),
+            )
+
+            shape = [P, 2, STEP_TILES, HEADS, PAIRS]
+            from_even = product_pool.tile(shape, F32)
+            from_odd = product_pool.tile(shape, F32)
+            for member, factors, product in ((0, even_factors, from_even), (1, odd_factors, from_odd)):
+                nc.vector.tensor_tensor(
+                    out=product[:],
+                    in0=rope[:, :, member, :]
+                    .rearrange("p t (h i) -> p t h i", h=HEADS)
+                    .unsqueeze(1)
+                    .to_broadcast(shape),
+                    in1=factors[:, step_in_batch].unsqueeze(3).to_broadcast(shape),
+                    op=MULT,
+                )
+            nc.gpsimd.tensor_tensor(
+                out=result[:, :, :, NOPE:HEAD_DIM].rearrange("p t h (i e) -> p t h i e", e=2),
+                in0=from_even[:].rearrange("p e t h i -> p t h i e"),
+                in1=from_odd[:].rearrange("p e t h i -> p t h i e"),
+                op=ADD,
+            )
+            j0 = step_in_batch * STEP_TILES
+            nc.sync.dma_start(
+                out=out_view[b, :, j0 : j0 + STEP_TILES, :],
+                in_=result[:].rearrange("p t h d -> p t (h d)"),
+            )
+
+        staged = transpose_and_quantise(0)
+        for step in range(STEPS):
+            following = transpose_and_quantise(step + 1) if step + 1 < STEPS else None
+            project_and_rotate(step, staged[0], staged[1])
+            staged = following

@@ -91,14 +91,12 @@ def tile_multilatentattention_pb_t_kernel(tc, hidden_states, rope_cos, rope_sin,
             in_=w_grouped[:].rearrange("q c t -> q (c t)"),
         )
 
-        even_factors = const.tile([P, STEPS_PER_BATCH, 2, STEP_TILES, PAIRS], BF16)
-        odd_factors = const.tile([P, STEPS_PER_BATCH, 2, STEP_TILES, PAIRS], BF16)
-        cos_by_step = cos_sb[:].rearrange("p (s t) i -> p s t i", t=STEP_TILES)
-        sin_by_step = sin_sb[:].rearrange("p (s t) i -> p s t i", t=STEP_TILES)
-        nc.vector.tensor_copy(out=even_factors[:, :, 0, :, :], in_=cos_by_step)
-        nc.vector.tensor_copy(out=even_factors[:, :, 1, :, :], in_=sin_by_step)
-        nc.vector.tensor_scalar_mul(out=odd_factors[:, :, 0, :, :], in0=sin_by_step, scalar1=-1.0)
-        nc.vector.tensor_copy(out=odd_factors[:, :, 1, :, :], in_=cos_by_step)
+        even_factors = const.tile([P, TILES_PER_BATCH, PAIRS, 2], BF16)
+        odd_factors = const.tile([P, TILES_PER_BATCH, PAIRS, 2], BF16)
+        nc.vector.tensor_copy(out=even_factors[:, :, :, 0], in_=cos_sb[:])
+        nc.vector.tensor_copy(out=even_factors[:, :, :, 1], in_=sin_sb[:])
+        nc.vector.tensor_scalar_mul(out=odd_factors[:, :, :, 0], in0=sin_sb[:], scalar1=-1.0)
+        nc.vector.tensor_copy(out=odd_factors[:, :, :, 1], in_=cos_sb[:])
 
         def transpose_and_quantise(step):
             words = x_tiles[step // STEPS_PER_LOAD][:].bitcast(F32)
@@ -149,7 +147,8 @@ def tile_multilatentattention_pb_t_kernel(tc, hidden_states, rope_cos, rope_sin,
                 in_=plain[:].rearrange("p t (h d) -> p t h d", h=HEADS),
             )
 
-            shape = [P, 2, STEP_TILES, HEADS, PAIRS]
+            j0 = step_in_batch * STEP_TILES
+            shape = [P, STEP_TILES, HEADS, PAIRS, 2]
             from_even = product_pool.tile(shape, F32)
             from_odd = product_pool.tile(shape, F32)
             for member, factors, product in ((0, even_factors, from_even), (1, odd_factors, from_odd)):
@@ -157,18 +156,17 @@ def tile_multilatentattention_pb_t_kernel(tc, hidden_states, rope_cos, rope_sin,
                     out=product[:],
                     in0=rope[:, :, member, :]
                     .rearrange("p t (h i) -> p t h i", h=HEADS)
-                    .unsqueeze(1)
+                    .unsqueeze(4)
                     .to_broadcast(shape),
-                    in1=factors[:, step_in_batch].unsqueeze(3).to_broadcast(shape),
+                    in1=factors[:, j0 : j0 + STEP_TILES].unsqueeze(2).to_broadcast(shape),
                     op=MULT,
                 )
             nc.gpsimd.tensor_tensor(
-                out=result[:, :, :, NOPE:HEAD_DIM].rearrange("p t h (i e) -> p t h i e", e=2),
-                in0=from_even[:].rearrange("p e t h i -> p t h i e"),
-                in1=from_odd[:].rearrange("p e t h i -> p t h i e"),
+                out=result[:, :, :, NOPE:HEAD_DIM],
+                in0=from_even[:].rearrange("p t h i e -> p t h (i e)"),
+                in1=from_odd[:].rearrange("p t h i e -> p t h (i e)"),
                 op=ADD,
             )
-            j0 = step_in_batch * STEP_TILES
             nc.sync.dma_start(
                 out=out_view[b, :, j0 : j0 + STEP_TILES, :],
                 in_=result[:].rearrange("p t h d -> p t (h d)"),

@@ -28,6 +28,7 @@ LOAD_TILES = 4
 STEPS_PER_LOAD = LOAD_TILES // STEP_TILES
 LOADS = BATCH * TILES_PER_BATCH // LOAD_TILES
 WORDS = HID // 2
+VECTOR_ADDS_EVERY = 8
 
 FLOPS = 2 * BATCH * TOKENS * HID * COLS
 
@@ -161,7 +162,8 @@ def tile_multilatentattention_pb_t_kernel(tc, hidden_states, rope_cos, rope_sin,
                     in1=factors[:, j0 : j0 + STEP_TILES].unsqueeze(2).to_broadcast(shape),
                     op=MULT,
                 )
-            nc.gpsimd.tensor_tensor(
+            adder = nc.vector if step % VECTOR_ADDS_EVERY == VECTOR_ADDS_EVERY - 1 else nc.gpsimd
+            adder.tensor_tensor(
                 out=result[:, :, :, NOPE:HEAD_DIM],
                 in0=from_even[:].rearrange("p t h i e -> p t h (i e)"),
                 in1=from_odd[:].rearrange("p t h i e -> p t h (i e)"),

@@ -28,7 +28,6 @@ LOAD_TILES = 4
 STEPS_PER_LOAD = LOAD_TILES // STEP_TILES
 LOADS = BATCH * TILES_PER_BATCH // LOAD_TILES
 WORDS = HID // 2
-VECTOR_ADDS_EVERY = 8
 
 FLOPS = 2 * BATCH * TOKENS * HID * COLS
 
@@ -37,6 +36,8 @@ def tile_multilatentattention_pb_t_kernel(tc, hidden_states, rope_cos, rope_sin,
     nc = tc.nc
     x_view = hidden_states.rearrange("b (p j) k -> b p j k", p=P)
     out_view = out.rearrange("b (p j) h d -> b p j (h d)", p=P)
+    PLAIN_SLICE = slice(0, PLAIN_COLS)
+    ROPE_SLICE = slice(PLAIN_COLS, COLS)
 
     with ExitStack() as ctx:
         const = ctx.enter_context(tc.tile_pool(name="const", bufs=1))
@@ -74,30 +75,23 @@ def tile_multilatentattention_pb_t_kernel(tc, hidden_states, rope_cos, rope_sin,
         make_identity(nc, ident[:])
 
         w_grouped = const.tile([P, COLS, PACK], BF16, align_bytes=64)
-        nc.vector.tensor_copy(
-            out=w_grouped[:, 0:PLAIN_COLS, :].rearrange("q (h d) t -> q h d t", h=HEADS),
-            in_=w_raw[:].rearrange("q t (h z d) -> q z h d t", h=HEADS, z=2)[:, 0],
-        )
+        w_codes = const.tile([P, COLS], U32, align_bytes=64)
+        w_scales = const.tile([P, COLS], U8, align_bytes=64)
+
+        def quantise_w(cols):
+            nc.vector.quantize_mx(
+                out=w_codes[:, cols].bitcast(FP8X4),
+                scales=w_scales[:, cols],
+                in_=w_grouped[:, cols, :].rearrange("q c t -> q (c t)"),
+            )
+
         for e in range(2):
             first = PLAIN_COLS + e * PLANE
             nc.vector.tensor_copy(
                 out=w_grouped[:, first : first + PLANE, :].rearrange("q (h i) t -> q h i t", h=HEADS),
                 in_=w_raw[:].rearrange("q t (h z i e) -> q z e h i t", h=HEADS, z=2, e=2)[:, 1, e],
             )
-        w_codes = const.tile([P, COLS], U32, align_bytes=64)
-        w_scales = const.tile([P, COLS], U8, align_bytes=64)
-        nc.vector.quantize_mx(
-            out=w_codes[:].bitcast(FP8X4),
-            scales=w_scales[:],
-            in_=w_grouped[:].rearrange("q c t -> q (c t)"),
-        )
-
-        even_factors = const.tile([P, TILES_PER_BATCH, PAIRS, 2], BF16)
-        odd_factors = const.tile([P, TILES_PER_BATCH, PAIRS, 2], BF16)
-        nc.vector.tensor_copy(out=even_factors[:, :, :, 0], in_=cos_sb[:])
-        nc.vector.tensor_copy(out=even_factors[:, :, :, 1], in_=sin_sb[:])
-        nc.vector.tensor_scalar_mul(out=odd_factors[:, :, :, 0], in0=sin_sb[:], scalar1=-1.0)
-        nc.vector.tensor_copy(out=odd_factors[:, :, :, 1], in_=cos_sb[:])
+        quantise_w(ROPE_SLICE)
 
         def transpose_and_quantise(step):
             words = x_tiles[step // STEPS_PER_LOAD][:].bitcast(F32)
@@ -117,30 +111,37 @@ def tile_multilatentattention_pb_t_kernel(tc, hidden_states, rope_cos, rope_sin,
             nc.vector.quantize_mx(out=x_codes[:].bitcast(FP8X4), scales=x_scales[:], in_=grouped[:])
             return x_codes, x_scales
 
+        staged = transpose_and_quantise(0)
+
+        even_factors = const.tile([P, TILES_PER_BATCH, PAIRS, 2], BF16)
+        odd_factors = const.tile([P, TILES_PER_BATCH, PAIRS, 2], BF16)
+        nc.vector.tensor_copy(out=even_factors[:, :, :, 0], in_=cos_sb[:])
+        nc.vector.tensor_copy(out=even_factors[:, :, :, 1], in_=sin_sb[:])
+        nc.vector.tensor_scalar_mul(out=odd_factors[:, :, :, 0], in0=sin_sb[:], scalar1=-1.0)
+        nc.vector.tensor_copy(out=odd_factors[:, :, :, 1], in_=cos_sb[:])
+
+        nc.scalar.copy(
+            out=w_grouped[:, PLAIN_SLICE, :].rearrange("q (h d) t -> q h d t", h=HEADS),
+            in_=w_raw[:].rearrange("q t (h z d) -> q z h d t", h=HEADS, z=2)[:, 0],
+        )
+        quantise_w(PLAIN_SLICE)
+
         def project_and_rotate(step, x_codes, x_scales):
             b, step_in_batch = divmod(step, STEPS_PER_BATCH)
             plain = plain_pool.tile([P, STEP_TILES, PLAIN_COLS], F32)
             rope = rope_pool.tile([P, STEP_TILES, 2, PLANE], F32)
-            for t in range(STEP_TILES):
-                tokens = slice(t * P, (t + 1) * P)
-                nc.tensor.matmul_mx(
-                    out=plain[:, t, :],
-                    lhsT=x_codes[:, tokens].bitcast(FP8X4),
-                    lhsT_scale=x_scales[:, tokens],
-                    rhs=w_codes[:, 0:PLAIN_COLS].bitcast(FP8X4),
-                    rhs_scale=w_scales[:, 0:PLAIN_COLS],
-                    start=True,
-                    stop=True,
-                )
-                nc.tensor.matmul_mx(
-                    out=rope[:, t, :, :].rearrange("p e c -> p (e c)"),
-                    lhsT=x_codes[:, tokens].bitcast(FP8X4),
-                    lhsT_scale=x_scales[:, tokens],
-                    rhs=w_codes[:, PLAIN_COLS:COLS].bitcast(FP8X4),
-                    rhs_scale=w_scales[:, PLAIN_COLS:COLS],
-                    start=True,
-                    stop=True,
-                )
+            for bank, cols in ((rope[:].rearrange("p t e c -> p t (e c)"), ROPE_SLICE), (plain[:], PLAIN_SLICE)):
+                for t in range(STEP_TILES):
+                    tokens = slice(t * P, (t + 1) * P)
+                    nc.tensor.matmul_mx(
+                        out=bank[:, t, :],
+                        lhsT=x_codes[:, tokens].bitcast(FP8X4),
+                        lhsT_scale=x_scales[:, tokens],
+                        rhs=w_codes[:, cols].bitcast(FP8X4),
+                        rhs_scale=w_scales[:, cols],
+                        start=True,
+                        stop=True,
+                    )
 
             result = out_pool.tile([P, STEP_TILES, HEADS, HEAD_DIM], F32)
             nc.scalar.copy(
@@ -162,7 +163,7 @@ def tile_multilatentattention_pb_t_kernel(tc, hidden_states, rope_cos, rope_sin,
                     in1=factors[:, j0 : j0 + STEP_TILES].unsqueeze(2).to_broadcast(shape),
                     op=MULT,
                 )
-            adder = nc.vector if step % VECTOR_ADDS_EVERY == VECTOR_ADDS_EVERY - 1 else nc.gpsimd
+            adder = nc.vector if step == STEPS - 1 else nc.gpsimd
             adder.tensor_tensor(
                 out=result[:, :, :, NOPE:HEAD_DIM],
                 in0=from_even[:].rearrange("p t h i e -> p t h (i e)"),
@@ -174,7 +175,6 @@ def tile_multilatentattention_pb_t_kernel(tc, hidden_states, rope_cos, rope_sin,
                 in_=result[:].rearrange("p t h d -> p t (h d)"),
             )
 
-        staged = transpose_and_quantise(0)
         for step in range(STEPS):
             following = transpose_and_quantise(step + 1) if step + 1 < STEPS else None
             project_and_rotate(step, staged[0], staged[1])

from contextlib import ExitStack

import concourse.mybir as mybir
from concourse.masks import make_identity

F32 = mybir.dt.float32
BF16 = mybir.dt.bfloat16
U32 = mybir.dt.uint32
U8 = mybir.dt.uint8
FP8X4 = mybir.dt.float8_e4m3fn_x4
MULT = mybir.AluOpType.mult
ADD = mybir.AluOpType.add

P = 128
PACK = 4
BATCH, TOKENS, HID = 4, 2048, 512
HEADS, HEAD_DIM = 4, 128
NOPE = 64
PAIRS = 32
COLS = HEADS * HEAD_DIM
PLAIN_COLS = HEADS * NOPE
PLANE = HEADS * PAIRS
TILES_PER_BATCH = TOKENS // P
STEP_TILES = 2
STEPS_PER_BATCH = TILES_PER_BATCH // STEP_TILES
STEPS = BATCH * STEPS_PER_BATCH
LOAD_TILES = 4
STEPS_PER_LOAD = LOAD_TILES // STEP_TILES
LOADS = BATCH * TILES_PER_BATCH // LOAD_TILES
WORDS = HID // 2

FLOPS = 2 * BATCH * TOKENS * HID * COLS


def tile_multilatentattention_pb_t_kernel(tc, hidden_states, rope_cos, rope_sin, Wq, out):
    nc = tc.nc
    x_view = hidden_states.rearrange("b (p j) k -> b p j k", p=P)
    out_view = out.rearrange("b (p j) h d -> b p j (h d)", p=P)
    PLAIN_SLICE = slice(0, PLAIN_COLS)
    ROPE_SLICE = slice(PLAIN_COLS, COLS)

    with ExitStack() as ctx:
        const = ctx.enter_context(tc.tile_pool(name="const", bufs=1))
        x_pool = ctx.enter_context(tc.tile_pool(name="x", bufs=LOADS))
        grouped_pool = ctx.enter_context(tc.tile_pool(name="grouped", bufs=3))
        mx_pool = ctx.enter_context(tc.tile_pool(name="mx", bufs=3))
        product_pool = ctx.enter_context(tc.tile_pool(name="product", bufs=3))
        out_pool = ctx.enter_context(tc.tile_pool(name="result", bufs=8))
        xt_pool = ctx.enter_context(tc.psum_pool(name="xt", bufs=2))
        plain_pool = ctx.enter_context(tc.psum_pool(name="plain", bufs=3))
        rope_pool = ctx.enter_context(tc.psum_pool(name="rope", bufs=3))

        def load_tokens(load):
            b, j0 = divmod(load * LOAD_TILES, TILES_PER_BATCH)
            x_sb = x_pool.tile([P, LOAD_TILES * HID], BF16)
            nc.sync.dma_start(
                out=x_sb[:], in_=x_view[b, :, j0 : j0 + LOAD_TILES, :].rearrange("p j k -> p (j k)")
            )
            return x_sb

        x_tiles = [load_tokens(0)]
        w_raw = const.tile([P, PACK, COLS], BF16)
        nc.sync.dma_start(
            out=w_raw[:].rearrange("q (u e) c -> q u e c", u=2),
            in_=Wq.rearrange("(u q e) c -> q u e c", u=2, e=2),
        )
        cos_sb = const.tile([P, TILES_PER_BATCH, PAIRS], BF16)
        nc.sync.dma_start(out=cos_sb[:], in_=rope_cos.rearrange("(p j) i -> p j i", p=P))
        sin_sb = const.tile([P, TILES_PER_BATCH, PAIRS], BF16)
        nc.sync.dma_start(out=sin_sb[:], in_=rope_sin.rearrange("(p j) i -> p j i", p=P))
        for load in range(1, LOADS):
            x_tiles.append(load_tokens(load))

        ident = const.tile([P, P], F32)
        make_identity(nc, ident[:])

        w_grouped = const.tile([P, COLS, PACK], BF16, align_bytes=64)
        w_codes = const.tile([P, COLS], U32, align_bytes=64)
        w_scales = const.tile([P, COLS], U8, align_bytes=64)

        def quantise_w(cols):
            nc.vector.quantize_mx(
                out=w_codes[:, cols].bitcast(FP8X4),
                scales=w_scales[:, cols],
                in_=w_grouped[:, cols, :].rearrange("q c t -> q (c t)"),
            )

        for e in range(2):
            first = PLAIN_COLS + e * PLANE
            nc.vector.tensor_copy(
                out=w_grouped[:, first : first + PLANE, :].rearrange("q (h i) t -> q h i t", h=HEADS),
                in_=w_raw[:].rearrange("q t (h z i e) -> q z e h i t", h=HEADS, z=2, e=2)[:, 1, e],
            )
        quantise_w(ROPE_SLICE)

        def transpose_and_quantise(step):
            words = x_tiles[step // STEPS_PER_LOAD][:].bitcast(F32)
            first_word = (step % STEPS_PER_LOAD) * STEP_TILES * WORDS
            xt = xt_pool.tile([P, STEP_TILES, 2, P], F32)
            for t in range(STEP_TILES):
                for u in range(2):
                    start = first_word + (2 * t + u) * P
                    nc.tensor.transpose(xt[:, t, u, :], words[:, start : start + P], ident[:])
            grouped = grouped_pool.tile([P, STEP_TILES * P * PACK], BF16, align_bytes=64)
            nc.scalar.copy(
                out=grouped[:].bitcast(F32).rearrange("q (t n u) -> q t n u", t=STEP_TILES, u=2),
                in_=xt[:].rearrange("q t u n -> q t n u"),
            )
            x_codes = mx_pool.tile([P, STEP_TILES * P], U32, align_bytes=64)
            x_scales = mx_pool.tile([P, STEP_TILES * P], U8, align_bytes=64)
            nc.vector.quantize_mx(out=x_codes[:].bitcast(FP8X4), scales=x_scales[:], in_=grouped[:])
            return x_codes, x_scales

        staged = transpose_and_quantise(0)

        even_factors = const.tile([P, TILES_PER_BATCH, PAIRS, 2], BF16)
        odd_factors = const.tile([P, TILES_PER_BATCH, PAIRS, 2], BF16)
        nc.vector.tensor_copy(out=even_factors[:, :, :, 0], in_=cos_sb[:])
        nc.vector.tensor_copy(out=even_factors[:, :, :, 1], in_=sin_sb[:])
        nc.vector.tensor_scalar_mul(out=odd_factors[:, :, :, 0], in0=sin_sb[:], scalar1=-1.0)
        nc.vector.tensor_copy(out=odd_factors[:, :, :, 1], in_=cos_sb[:])

        nc.scalar.copy(
            out=w_grouped[:, PLAIN_SLICE, :].rearrange("q (h d) t -> q h d t", h=HEADS),
            in_=w_raw[:].rearrange("q t (h z d) -> q z h d t", h=HEADS, z=2)[:, 0],
        )
        quantise_w(PLAIN_SLICE)

        def project_and_rotate(step, x_codes, x_scales):
            b, step_in_batch = divmod(step, STEPS_PER_BATCH)
            plain = plain_pool.tile([P, STEP_TILES, PLAIN_COLS], F32)
            rope = rope_pool.tile([P, STEP_TILES, 2, PLANE], F32)
            for bank, cols in ((rope[:].rearrange("p t e c -> p t (e c)"), ROPE_SLICE), (plain[:], PLAIN_SLICE)):
                for t in range(STEP_TILES):
                    tokens = slice(t * P, (t + 1) * P)
                    nc.tensor.matmul_mx(
                        out=bank[:, t, :],
                        lhsT=x_codes[:, tokens].bitcast(FP8X4),
                        lhsT_scale=x_scales[:, tokens],
                        rhs=w_codes[:, cols].bitcast(FP8X4),
                        rhs_scale=w_scales[:, cols],
                        start=True,
                        stop=True,
                    )

            result = out_pool.tile([P, STEP_TILES, HEADS, HEAD_DIM], F32)
            nc.scalar.copy(
                out=result[:, :, :, 0:NOPE],
                in_=plain[:].rearrange("p t (h d) -> p t h d", h=HEADS),
            )

            j0 = step_in_batch * STEP_TILES
            shape = [P, STEP_TILES, HEADS, PAIRS, 2]
            from_even = product_pool.tile(shape, F32)
            from_odd = product_pool.tile(shape, F32)
            for member, factors, product in ((0, even_factors, from_even), (1, odd_factors, from_odd)):
                nc.vector.tensor_tensor(
                    out=product[:],
                    in0=rope[:, :, member, :]
                    .rearrange("p t (h i) -> p t h i", h=HEADS)
                    .unsqueeze(4)
                    .to_broadcast(shape),
                    in1=factors[:, j0 : j0 + STEP_TILES].unsqueeze(2).to_broadcast(shape),
                    op=MULT,
                )
            adder = nc.vector if step == STEPS - 1 else nc.gpsimd
            adder.tensor_tensor(
                out=result[:, :, :, NOPE:HEAD_DIM],
                in0=from_even[:].rearrange("p t h i e -> p t h (i e)"),
                in1=from_odd[:].rearrange("p t h i e -> p t h (i e)"),
                op=ADD,
            )
            nc.sync.dma_start(
                out=out_view[b, :, j0 : j0 + STEP_TILES, :],
                in_=result[:].rearrange("p t h d -> p t (h d)"),
            )

        for step in range(STEPS):
            following = transpose_and_quantise(step + 1) if step + 1 < STEPS else None
            project_and_rotate(step, staged[0], staged[1])
            staged = following
